import numpy as np
import ml_dtypes

BF16 = ml_dtypes.bfloat16


def bf(x):
    return np.asarray(x, np.float32).astype(BF16)


def f32(x):
    return np.asarray(x, np.float32)


def f64(x):
    return np.asarray(x).astype(np.float64)


def striped(idx):
    return np.tile(idx.reshape(-1, 16).T, (8, 1))


C, S, N, E = 1024, 256, 128, 256


def setup_inputs():
    return {"base": f32(np.random.standard_normal((C, S))), "x": bf(np.random.standard_normal((E, N))), "w": bf(np.random.standard_normal((E, C)) / np.sqrt(E)), "b": f32(0.1 * np.random.standard_normal((C, 1))), "offs": striped(np.random.permutation(S)[:N])}


def reference(base, x, w, b, offs):
    idx = offs[:16].T.reshape(-1)
    v = f64(w).T @ f64(x) + f64(b)
    out = f64(base).copy()
    out[:, idx] = np.maximum(v, 0.0) + (np.exp(np.minimum(v, 0.0)) - 1.0)
    return out

@@ -1,0 +1,71 @@
+import concourse.mybir as mybir
+
+F32 = mybir.dt.float32
+BF16 = mybir.dt.bfloat16
+U16 = mybir.dt.uint16
+ACT = mybir.ActivationFunctionType
+ALU = mybir.AluOpType
+
+P = 128
+C, S, N, E = 1024, 256, 128, 256
+BLOCKS = C // P
+HALVES = E // P
+
+FLOPS = 2 * E * C * N
+
+
+def tile_mthisan_kernel(tc, base, x, w, b, offs, out):
+    nc = tc.nc
+
+    base_blocks = base.rearrange("(p k) s -> p k s", k=BLOCKS)
+    out_blocks = out.rearrange("(p k) s -> p k s", k=BLOCKS)
+
+    with (
+        tc.tile_pool(name="held", bufs=1) as held,
+        tc.tile_pool(name="work", bufs=3) as work,
+        tc.psum_pool(name="psum", bufs=4) as psum,
+    ):
+        offsets = held.tile([P, N // 16], U16, name="offsets")
+        nc.sync.dma_start(offsets[:], offs)
+
+        x_sb = held.tile([P, HALVES, N], BF16, name="x_sb")
+        nc.sync.dma_start(x_sb[:], x.rearrange("(h p) n -> p h n", p=P))
+        w_sb = held.tile([P, HALVES, C], BF16, name="w_sb")
+        nc.sync.dma_start(w_sb[:], w.rearrange("(h p) c -> p h c", p=P))
+        w_blocks = w_sb[:].rearrange("p h (m k) -> p h k m", k=BLOCKS)
+
+        bias = held.tile([P, BLOCKS], F32, name="bias")
+        nc.scalar.dma_start(bias[:], b.rearrange("(p k) o -> p (k o)", k=BLOCKS))
+        minus_bias = held.tile([P, BLOCKS], F32, name="minus_bias")
+        nc.vector.tensor_scalar_mul(minus_bias[:], bias[:], -1.0)
+
+        windows = [held.tile([P, S], F32, name=f"window{k}") for k in range(BLOCKS)]
+        for k in range(BLOCKS):
+            nc.scalar.dma_start(windows[k][:], base_blocks[:, k, :])
+
+        for k in range(BLOCKS):
+            product = psum.tile([P, N], F32, name="product")
+            for h in range(HALVES):
+                nc.tensor.matmul(
+                    product[:],
+                    w_blocks[:, h, k, :],
+                    x_sb[:, h, :],
+                    start=(h == 0),
+                    stop=(h == HALVES - 1),
+                )
+
+            minus_min = work.tile([P, N], F32, name="minus_min")
+            nc.scalar.activation(
+                minus_min[:], product[:], ACT.Relu, bias=minus_bias[:, k : k + 1], scale=-1.0
+            )
+            exp_min = work.tile([P, N], F32, name="exp_min")
+            nc.scalar.activation(exp_min[:], minus_min[:], ACT.Exp, scale=-1.0)
+            negative_part = work.tile([P, N], F32, name="negative_part")
+            nc.gpsimd.tensor_scalar_add(negative_part[:], exp_min[:], -1.0)
+            positive_part = work.tile([P, N], F32, name="positive_part")
+            nc.scalar.activation(positive_part[:], product[:], ACT.Relu, bias=bias[:, k : k + 1])
+
+            nc.vector.tensor_tensor(
+                windows[k][:].indirect(offsets[:]), positive_part[:], negative_part[:], ALU.add
+            )
+            nc.sync.dma_start(out_blocks[:, k, :], windows[k][:])

@@ -61,9 +61,9 @@ def tile_mthisan_kernel(tc, base, x, w, b, offs, out):
             exp_min = work.tile([P, N], F32, name="exp_min")
             nc.scalar.activation(exp_min[:], minus_min[:], ACT.Exp, scale=-1.0)
             negative_part = work.tile([P, N], F32, name="negative_part")
-            nc.gpsimd.tensor_scalar_add(negative_part[:], exp_min[:], -1.0)
             positive_part = work.tile([P, N], F32, name="positive_part")
             nc.scalar.activation(positive_part[:], product[:], ACT.Relu, bias=bias[:, k : k + 1])
+            nc.scalar.activation(negative_part[:], exp_min[:], ACT.Copy, bias=-1.0)
 
             nc.vector.tensor_tensor(
                 windows[k][:].indirect(offsets[:]), positive_part[:], negative_part[:], ALU.add

@@ -28,20 +28,27 @@ def tile_mthisan_kernel(tc, base, x, w, b, offs, out):
         offsets = held.tile([P, N // 16], U16, name="offsets")
         nc.sync.dma_start(offsets[:], offs)
 
+        scratch = held.tile([P, 1], F32, name="scratch")
+        nc.vector.memset(scratch[:], 0.0)
+        warmed = held.tile([P, 1], F32, name="warmed")
+        nc.scalar.activation(warmed[:], scratch[:], ACT.Exp)
+
         x_sb = held.tile([P, HALVES, N], BF16, name="x_sb")
         nc.sync.dma_start(x_sb[:], x.rearrange("(h p) n -> p h n", p=P))
         w_sb = held.tile([P, HALVES, C], BF16, name="w_sb")
-        nc.sync.dma_start(w_sb[:], w.rearrange("(h p) c -> p h c", p=P))
-        w_blocks = w_sb[:].rearrange("p h (m k) -> p h k m", k=BLOCKS)
-
+        w_halves = w.rearrange("(h p) c -> p h c", p=P)
+        nc.sync.dma_start(w_sb[:, 0, :], w_halves[:, 0, :])
         bias = held.tile([P, BLOCKS], F32, name="bias")
         nc.scalar.dma_start(bias[:], b.rearrange("(p k) o -> p (k o)", k=BLOCKS))
+        nc.scalar.dma_start(w_sb[:, 1, :], w_halves[:, 1, :])
+        w_blocks = w_sb[:].rearrange("p h (m k) -> p h k m", k=BLOCKS)
+
         minus_bias = held.tile([P, BLOCKS], F32, name="minus_bias")
         nc.vector.tensor_scalar_mul(minus_bias[:], bias[:], -1.0)
 
         windows = [held.tile([P, S], F32, name=f"window{k}") for k in range(BLOCKS)]
         for k in range(BLOCKS):
-            nc.scalar.dma_start(windows[k][:], base_blocks[:, k, :])
+            nc.sync.dma_start(windows[k][:], base_blocks[:, k, :])
 
         for k in range(BLOCKS):
             product = psum.tile([P, N], F32, name="product")

@@ -50,7 +50,7 @@ def tile_mthisan_kernel(tc, base, x, w, b, offs, out):
         for k in range(BLOCKS):
             nc.sync.dma_start(windows[k][:], base_blocks[:, k, :])
 
-        for k in range(BLOCKS):
+        def open_block(k):
             product = psum.tile([P, N], F32, name="product")
             for h in range(HALVES):
                 nc.tensor.matmul(
@@ -60,16 +60,22 @@ def tile_mthisan_kernel(tc, base, x, w, b, offs, out):
                     start=(h == 0),
                     stop=(h == HALVES - 1),
                 )
-
             minus_min = work.tile([P, N], F32, name="minus_min")
             nc.scalar.activation(
                 minus_min[:], product[:], ACT.Relu, bias=minus_bias[:, k : k + 1], scale=-1.0
             )
-            exp_min = work.tile([P, N], F32, name="exp_min")
-            nc.scalar.activation(exp_min[:], minus_min[:], ACT.Exp, scale=-1.0)
-            negative_part = work.tile([P, N], F32, name="negative_part")
             positive_part = work.tile([P, N], F32, name="positive_part")
             nc.scalar.activation(positive_part[:], product[:], ACT.Relu, bias=bias[:, k : k + 1])
+            return positive_part, minus_min
+
+        opened = open_block(0)
+        for k in range(BLOCKS):
+            positive_part, minus_min = opened
+            exp_min = work.tile([P, N], F32, name="exp_min")
+            nc.scalar.activation(exp_min[:], minus_min[:], ACT.Exp, scale=-1.0)
+            if k + 1 < BLOCKS:
+                opened = open_block(k + 1)
+            negative_part = work.tile([P, N], F32, name="negative_part")
             nc.scalar.activation(negative_part[:], exp_min[:], ACT.Copy, bias=-1.0)
 
             nc.vector.tensor_tensor(

@@ -8,8 +8,10 @@ ALU = mybir.AluOpType
 
 P = 128
 C, S, N, E = 1024, 256, 128, 256
-BLOCKS = C // P
 HALVES = E // P
+GROUPS = 2
+BLOCKS = C // P // GROUPS
+GROUP_C = C // GROUPS
 
 FLOPS = 2 * E * C * N
 
@@ -17,8 +19,9 @@ FLOPS = 2 * E * C * N
 def tile_mthisan_kernel(tc, base, x, w, b, offs, out):
     nc = tc.nc
 
-    base_blocks = base.rearrange("(p k) s -> p k s", k=BLOCKS)
-    out_blocks = out.rearrange("(p k) s -> p k s", k=BLOCKS)
+    base_blocks = base.rearrange("(g p i) s -> p g i s", g=GROUPS, i=BLOCKS)
+    out_blocks = out.rearrange("(g p i) s -> p g i s", g=GROUPS, i=BLOCKS)
+    w_groups = w.rearrange("(h p) (g c) -> p h g c", p=P, g=GROUPS)
 
     with (
         tc.tile_pool(name="held", bufs=1) as held,
@@ -27,58 +30,60 @@ def tile_mthisan_kernel(tc, base, x, w, b, offs, out):
     ):
         offsets = held.tile([P, N // 16], U16, name="offsets")
         nc.sync.dma_start(offsets[:], offs)
+        x_sb = held.tile([P, HALVES, N], BF16, name="x_sb")
+        nc.sync.dma_start(x_sb[:], x.rearrange("(h p) n -> p h n", p=P))
+        bias = held.tile([P, GROUPS, BLOCKS], F32, name="bias")
+        nc.scalar.dma_start(bias[:], b.rearrange("(g p i) o -> p g (i o)", g=GROUPS, i=BLOCKS))
+
+        w_sb = [held.tile([P, HALVES, GROUP_C], BF16, name=f"w_sb{g}") for g in range(GROUPS)]
+        windows = [
+            [held.tile([P, S], F32, name=f"window{g}_{i}") for i in range(BLOCKS)]
+            for g in range(GROUPS)
+        ]
+        for g in range(GROUPS):
+            nc.sync.dma_start(w_sb[g][:, 0, :], w_groups[:, 0, g, :])
+            nc.scalar.dma_start(w_sb[g][:, 1, :], w_groups[:, 1, g, :])
+            for i in range(BLOCKS):
+                nc.sync.dma_start(windows[g][i][:], base_blocks[:, g, i, :])
 
         scratch = held.tile([P, 1], F32, name="scratch")
         nc.vector.memset(scratch[:], 0.0)
         warmed = held.tile([P, 1], F32, name="warmed")
         nc.scalar.activation(warmed[:], scratch[:], ACT.Exp)
 
-        x_sb = held.tile([P, HALVES, N], BF16, name="x_sb")
-        nc.sync.dma_start(x_sb[:], x.rearrange("(h p) n -> p h n", p=P))
-        w_sb = held.tile([P, HALVES, C], BF16, name="w_sb")
-        w_halves = w.rearrange("(h p) c -> p h c", p=P)
-        nc.sync.dma_start(w_sb[:, 0, :], w_halves[:, 0, :])
-        bias = held.tile([P, BLOCKS], F32, name="bias")
-        nc.scalar.dma_start(bias[:], b.rearrange("(p k) o -> p (k o)", k=BLOCKS))
-        nc.scalar.dma_start(w_sb[:, 1, :], w_halves[:, 1, :])
-        w_blocks = w_sb[:].rearrange("p h (m k) -> p h k m", k=BLOCKS)
-
-        minus_bias = held.tile([P, BLOCKS], F32, name="minus_bias")
+        minus_bias = held.tile([P, GROUPS, BLOCKS], F32, name="minus_bias")
         nc.vector.tensor_scalar_mul(minus_bias[:], bias[:], -1.0)
 
-        windows = [held.tile([P, S], F32, name=f"window{k}") for k in range(BLOCKS)]
-        for k in range(BLOCKS):
-            nc.sync.dma_start(windows[k][:], base_blocks[:, k, :])
+        for g in range(GROUPS):
+            w_blocks = w_sb[g][:].rearrange("p h (m i) -> p h i m", i=BLOCKS)
+            for i in range(BLOCKS):
+                product = psum.tile([P, N], F32, name="product")
+                for h in range(HALVES):
+                    nc.tensor.matmul(
+                        product[:],
+                        w_blocks[:, h, i, :],
+                        x_sb[:, h, :],
+                        start=(h == 0),
+                        stop=(h == HALVES - 1),
+                    )
 
-        def open_block(k):
-            product = psum.tile([P, N], F32, name="product")
-            for h in range(HALVES):
-                nc.tensor.matmul(
-                    product[:],
-                    w_blocks[:, h, k, :],
-                    x_sb[:, h, :],
-                    start=(h == 0),
-                    stop=(h == HALVES - 1),
+                minus_min = work.tile([P, N], F32, name="minus_min")
+                nc.scalar.activation(
+                    minus_min[:], product[:], ACT.Relu, bias=minus_bias[:, g, i : i + 1], scale=-1.0
                 )
-            minus_min = work.tile([P, N], F32, name="minus_min")
-            nc.scalar.activation(
-                minus_min[:], product[:], ACT.Relu, bias=minus_bias[:, k : k + 1], scale=-1.0
-            )
-            positive_part = work.tile([P, N], F32, name="positive_part")
-            nc.scalar.activation(positive_part[:], product[:], ACT.Relu, bias=bias[:, k : k + 1])
-            return positive_part, minus_min
+                exp_min = work.tile([P, N], F32, name="exp_min")
+                nc.scalar.activation(exp_min[:], minus_min[:], ACT.Exp, scale=-1.0)
+                positive_part = work.tile([P, N], F32, name="positive_part")
+                nc.scalar.activation(
+                    positive_part[:], product[:], ACT.Relu, bias=bias[:, g, i : i + 1]
+                )
+                negative_part = work.tile([P, N], F32, name="negative_part")
+                nc.scalar.activation(negative_part[:], exp_min[:], ACT.Copy, bias=-1.0)
 
-        opened = open_block(0)
-        for k in range(BLOCKS):
-            positive_part, minus_min = opened
-            exp_min = work.tile([P, N], F32, name="exp_min")
-            nc.scalar.activation(exp_min[:], minus_min[:], ACT.Exp, scale=-1.0)
-            if k + 1 < BLOCKS:
-                opened = open_block(k + 1)
-            negative_part = work.tile([P, N], F32, name="negative_part")
-            nc.scalar.activation(negative_part[:], exp_min[:], ACT.Copy, bias=-1.0)
-
-            nc.vector.tensor_tensor(
-                windows[k][:].indirect(offsets[:]), positive_part[:], negative_part[:], ALU.add
-            )
-            nc.sync.dma_start(out_blocks[:, k, :], windows[k][:])
+                nc.vector.tensor_tensor(
+                    windows[g][i][:].indirect(offsets[:]),
+                    positive_part[:],
+                    negative_part[:],
+                    ALU.add,
+                )
+                nc.sync.dma_start(out_blocks[:, g, i, :], windows[g][i][:])

@@ -9,7 +9,7 @@ ALU = mybir.AluOpType
 P = 128
 C, S, N, E = 1024, 256, 128, 256
 HALVES = E // P
-GROUPS = 2
+GROUPS = 4
 BLOCKS = C // P // GROUPS
 GROUP_C = C // GROUPS
 
@@ -22,6 +22,7 @@ def tile_mthisan_kernel(tc, base, x, w, b, offs, out):
     base_blocks = base.rearrange("(g p i) s -> p g i s", g=GROUPS, i=BLOCKS)
     out_blocks = out.rearrange("(g p i) s -> p g i s", g=GROUPS, i=BLOCKS)
     w_groups = w.rearrange("(h p) (g c) -> p h g c", p=P, g=GROUPS)
+    x_halves = x.rearrange("(h p) n -> p h n", p=P)
 
     with (
         tc.tile_pool(name="held", bufs=1) as held,
@@ -29,22 +30,26 @@ def tile_mthisan_kernel(tc, base, x, w, b, offs, out):
         tc.psum_pool(name="psum", bufs=4) as psum,
     ):
         offsets = held.tile([P, N // 16], U16, name="offsets")
-        nc.sync.dma_start(offsets[:], offs)
         x_sb = held.tile([P, HALVES, N], BF16, name="x_sb")
-        nc.sync.dma_start(x_sb[:], x.rearrange("(h p) n -> p h n", p=P))
         bias = held.tile([P, GROUPS, BLOCKS], F32, name="bias")
-        nc.scalar.dma_start(bias[:], b.rearrange("(g p i) o -> p g (i o)", g=GROUPS, i=BLOCKS))
-
         w_sb = [held.tile([P, HALVES, GROUP_C], BF16, name=f"w_sb{g}") for g in range(GROUPS)]
         windows = [
             [held.tile([P, S], F32, name=f"window{g}_{i}") for i in range(BLOCKS)]
             for g in range(GROUPS)
         ]
+
+        queues = [nc.sync, nc.scalar]
+        for h in range(HALVES):
+            queues[h].dma_start(x_sb[:, h, :], x_halves[:, h, :])
+            queues[h].dma_start(w_sb[0][:, h, :], w_groups[:, h, 0, :])
+        nc.scalar.dma_start(bias[:], b.rearrange("(g p i) o -> p g (i o)", g=GROUPS, i=BLOCKS))
+        nc.sync.dma_start(offsets[:], offs)
         for g in range(GROUPS):
-            nc.sync.dma_start(w_sb[g][:, 0, :], w_groups[:, 0, g, :])
-            nc.scalar.dma_start(w_sb[g][:, 1, :], w_groups[:, 1, g, :])
             for i in range(BLOCKS):
                 nc.sync.dma_start(windows[g][i][:], base_blocks[:, g, i, :])
+            if g + 1 < GROUPS:
+                for h in range(HALVES):
+                    queues[h].dma_start(w_sb[g + 1][:, h, :], w_groups[:, h, g + 1, :])
 
         scratch = held.tile([P, 1], F32, name="scratch")
         nc.vector.memset(scratch[:], 0.0)

@@ -38,18 +38,16 @@ def tile_mthisan_kernel(tc, base, x, w, b, offs, out):
             for g in range(GROUPS)
         ]
 
-        queues = [nc.sync, nc.scalar]
-        for h in range(HALVES):
-            queues[h].dma_start(x_sb[:, h, :], x_halves[:, h, :])
-            queues[h].dma_start(w_sb[0][:, h, :], w_groups[:, h, 0, :])
+        nc.sync.dma_start(x_sb[:], x_halves)
+        nc.scalar.dma_start(w_sb[0][:], w_groups[:, :, 0, :])
         nc.scalar.dma_start(bias[:], b.rearrange("(g p i) o -> p g (i o)", g=GROUPS, i=BLOCKS))
         nc.sync.dma_start(offsets[:], offs)
+        nc.scalar.dma_start(w_sb[1][:], w_groups[:, :, 1, :])
         for g in range(GROUPS):
             for i in range(BLOCKS):
                 nc.sync.dma_start(windows[g][i][:], base_blocks[:, g, i, :])
-            if g + 1 < GROUPS:
-                for h in range(HALVES):
-                    queues[h].dma_start(w_sb[g + 1][:, h, :], w_groups[:, h, g + 1, :])
+                if i == 0 and 2 <= g + 1 < GROUPS:
+                    nc.sync.dma_start(w_sb[g + 1][:], w_groups[:, :, g + 1, :])
 
         scratch = held.tile([P, 1], F32, name="scratch")
         nc.vector.memset(scratch[:], 0.0)

@@ -9,7 +9,7 @@ ALU = mybir.AluOpType
 P = 128
 C, S, N, E = 1024, 256, 128, 256
 HALVES = E // P
-GROUPS = 4
+GROUPS = 2
 BLOCKS = C // P // GROUPS
 GROUP_C = C // GROUPS
 
@@ -22,7 +22,6 @@ def tile_mthisan_kernel(tc, base, x, w, b, offs, out):
     base_blocks = base.rearrange("(g p i) s -> p g i s", g=GROUPS, i=BLOCKS)
     out_blocks = out.rearrange("(g p i) s -> p g i s", g=GROUPS, i=BLOCKS)
     w_groups = w.rearrange("(h p) (g c) -> p h g c", p=P, g=GROUPS)
-    x_halves = x.rearrange("(h p) n -> p h n", p=P)
 
     with (
         tc.tile_pool(name="held", bufs=1) as held,
@@ -38,16 +37,16 @@ def tile_mthisan_kernel(tc, base, x, w, b, offs, out):
             for g in range(GROUPS)
         ]
 
-        nc.sync.dma_start(x_sb[:], x_halves)
-        nc.scalar.dma_start(w_sb[0][:], w_groups[:, :, 0, :])
+        nc.sync.dma_start(x_sb[:], x.rearrange("(h p) n -> p h n", p=P))
         nc.scalar.dma_start(bias[:], b.rearrange("(g p i) o -> p g (i o)", g=GROUPS, i=BLOCKS))
+        nc.sync.dma_start(w_sb[0][:, 0, :], w_groups[:, 0, 0, :])
+        nc.scalar.dma_start(w_sb[0][:, 1, :], w_groups[:, 1, 0, :])
         nc.sync.dma_start(offsets[:], offs)
-        nc.scalar.dma_start(w_sb[1][:], w_groups[:, :, 1, :])
         for g in range(GROUPS):
+            if g > 0:
+                nc.sync.dma_start(w_sb[g][:], w_groups[:, :, g, :])
             for i in range(BLOCKS):
                 nc.sync.dma_start(windows[g][i][:], base_blocks[:, g, i, :])
-                if i == 0 and 2 <= g + 1 < GROUPS:
-                    nc.sync.dma_start(w_sb[g + 1][:], w_groups[:, :, g + 1, :])
 
         scratch = held.tile([P, 1], F32, name="scratch")
         nc.vector.memset(scratch[:], 0.0)

@@ -69,18 +69,28 @@ def tile_mthisan_kernel(tc, base, x, w, b, offs, out):
                         stop=(h == HALVES - 1),
                     )
 
-                minus_min = work.tile([P, N], F32, name="minus_min")
-                nc.scalar.activation(
-                    minus_min[:], product[:], ACT.Relu, bias=minus_bias[:, g, i : i + 1], scale=-1.0
-                )
-                exp_min = work.tile([P, N], F32, name="exp_min")
-                nc.scalar.activation(exp_min[:], minus_min[:], ACT.Exp, scale=-1.0)
                 positive_part = work.tile([P, N], F32, name="positive_part")
-                nc.scalar.activation(
-                    positive_part[:], product[:], ACT.Relu, bias=bias[:, g, i : i + 1]
-                )
                 negative_part = work.tile([P, N], F32, name="negative_part")
-                nc.scalar.activation(negative_part[:], exp_min[:], ACT.Copy, bias=-1.0)
+                if g == 0 and i == 0:
+                    exp_v = work.tile([P, N], F32, name="exp_v")
+                    nc.scalar.activation(exp_v[:], product[:], ACT.Exp, bias=bias[:, g, i : i + 1])
+                    nc.scalar.activation(
+                        positive_part[:], product[:], ACT.Relu, bias=bias[:, g, i : i + 1]
+                    )
+                    nc.vector.tensor_scalar(
+                        negative_part[:], exp_v[:], 1.0, -1.0, op0=ALU.min, op1=ALU.add
+                    )
+                else:
+                    minus_min = work.tile([P, N], F32, name="minus_min")
+                    nc.scalar.activation(
+                        minus_min[:], product[:], ACT.Relu, bias=minus_bias[:, g, i : i + 1], scale=-1.0
+                    )
+                    exp_min = work.tile([P, N], F32, name="exp_min")
+                    nc.scalar.activation(exp_min[:], minus_min[:], ACT.Exp, scale=-1.0)
+                    nc.scalar.activation(
+                        positive_part[:], product[:], ACT.Relu, bias=bias[:, g, i : i + 1]
+                    )
+                    nc.scalar.activation(negative_part[:], exp_min[:], ACT.Copy, bias=-1.0)
 
                 nc.vector.tensor_tensor(
                     windows[g][i][:].indirect(offsets[:]),

@@ -9,7 +9,7 @@ ALU = mybir.AluOpType
 P = 128
 C, S, N, E = 1024, 256, 128, 256
 HALVES = E // P
-GROUPS = 2
+GROUPS = 4
 BLOCKS = C // P // GROUPS
 GROUP_C = C // GROUPS
 
@@ -21,12 +21,12 @@ def tile_mthisan_kernel(tc, base, x, w, b, offs, out):
 
     base_blocks = base.rearrange("(g p i) s -> p g i s", g=GROUPS, i=BLOCKS)
     out_blocks = out.rearrange("(g p i) s -> p g i s", g=GROUPS, i=BLOCKS)
-    w_groups = w.rearrange("(h p) (g c) -> p h g c", p=P, g=GROUPS)
+    w_groups = w.rearrange("(p h) (g c) -> p h g c", p=P, g=GROUPS)
 
     with (
         tc.tile_pool(name="held", bufs=1) as held,
-        tc.tile_pool(name="work", bufs=3) as work,
-        tc.psum_pool(name="psum", bufs=4) as psum,
+        tc.tile_pool(name="work", bufs=C // P) as work,
+        tc.psum_pool(name="psum", bufs=C // P) as psum,
     ):
         offsets = held.tile([P, N // 16], U16, name="offsets")
         x_sb = held.tile([P, HALVES, N], BF16, name="x_sb")
@@ -37,10 +37,9 @@ def tile_mthisan_kernel(tc, base, x, w, b, offs, out):
             for g in range(GROUPS)
         ]
 
-        nc.sync.dma_start(x_sb[:], x.rearrange("(h p) n -> p h n", p=P))
+        nc.sync.dma_start(w_sb[0][:], w_groups[:, :, 0, :])
+        nc.scalar.dma_start(x_sb[:], x.rearrange("(p h) n -> p h n", p=P))
         nc.scalar.dma_start(bias[:], b.rearrange("(g p i) o -> p g (i o)", g=GROUPS, i=BLOCKS))
-        nc.sync.dma_start(w_sb[0][:, 0, :], w_groups[:, 0, 0, :])
-        nc.scalar.dma_start(w_sb[0][:, 1, :], w_groups[:, 1, 0, :])
         nc.sync.dma_start(offsets[:], offs)
         for g in range(GROUPS):
             if g > 0:

@@ -9,9 +9,9 @@ ALU = mybir.AluOpType
 P = 128
 C, S, N, E = 1024, 256, 128, 256
 HALVES = E // P
-GROUPS = 4
-BLOCKS = C // P // GROUPS
-GROUP_C = C // GROUPS
+ALL_BLOCKS = C // P
+GROUP_BLOCKS = (2, 6)
+GROUPS = len(GROUP_BLOCKS)
 
 FLOPS = 2 * E * C * N
 
@@ -19,45 +19,47 @@ FLOPS = 2 * E * C * N
 def tile_mthisan_kernel(tc, base, x, w, b, offs, out):
     nc = tc.nc
 
-    base_blocks = base.rearrange("(g p i) s -> p g i s", g=GROUPS, i=BLOCKS)
-    out_blocks = out.rearrange("(g p i) s -> p g i s", g=GROUPS, i=BLOCKS)
-    w_groups = w.rearrange("(p h) (g c) -> p h g c", p=P, g=GROUPS)
+    first = [P * sum(GROUP_BLOCKS[:g]) for g in range(GROUPS + 1)]
+    w_rows = w.rearrange("(p h) c -> p h c", p=P)
+
+    def rows_of_group(array, g):
+        return array[first[g] : first[g + 1], :].rearrange("(p i) s -> p i s", p=P)
 
     with (
         tc.tile_pool(name="held", bufs=1) as held,
-        tc.tile_pool(name="work", bufs=C // P) as work,
-        tc.psum_pool(name="psum", bufs=C // P) as psum,
+        tc.tile_pool(name="work", bufs=ALL_BLOCKS) as work,
+        tc.psum_pool(name="psum", bufs=ALL_BLOCKS) as psum,
     ):
         offsets = held.tile([P, N // 16], U16, name="offsets")
         x_sb = held.tile([P, HALVES, N], BF16, name="x_sb")
-        bias = held.tile([P, GROUPS, BLOCKS], F32, name="bias")
-        w_sb = [held.tile([P, HALVES, GROUP_C], BF16, name=f"w_sb{g}") for g in range(GROUPS)]
+        bias = [held.tile([P, GROUP_BLOCKS[g]], F32, name=f"bias{g}") for g in range(GROUPS)]
+        w_sb = [
+            held.tile([P, HALVES, P * GROUP_BLOCKS[g]], BF16, name=f"w_sb{g}")
+            for g in range(GROUPS)
+        ]
         windows = [
-            [held.tile([P, S], F32, name=f"window{g}_{i}") for i in range(BLOCKS)]
+            [held.tile([P, S], F32, name=f"window{g}_{i}") for i in range(GROUP_BLOCKS[g])]
             for g in range(GROUPS)
         ]
 
-        nc.sync.dma_start(w_sb[0][:], w_groups[:, :, 0, :])
+        nc.sync.dma_start(w_sb[0][:], w_rows[:, :, first[0] : first[1]])
         nc.scalar.dma_start(x_sb[:], x.rearrange("(p h) n -> p h n", p=P))
-        nc.scalar.dma_start(bias[:], b.rearrange("(g p i) o -> p g (i o)", g=GROUPS, i=BLOCKS))
+        nc.scalar.dma_start(bias[0][:], rows_of_group(b, 0).rearrange("p i o -> p (i o)"))
         nc.sync.dma_start(offsets[:], offs)
+        nc.sync.dma_start(w_sb[1][:], w_rows[:, :, first[1] : first[2]])
+        nc.scalar.dma_start(bias[1][:], rows_of_group(b, 1).rearrange("p i o -> p (i o)"))
         for g in range(GROUPS):
-            if g > 0:
-                nc.sync.dma_start(w_sb[g][:], w_groups[:, :, g, :])
-            for i in range(BLOCKS):
-                nc.sync.dma_start(windows[g][i][:], base_blocks[:, g, i, :])
+            for i in range(GROUP_BLOCKS[g]):
+                nc.sync.dma_start(windows[g][i][:], rows_of_group(base, g)[:, i, :])
 
         scratch = held.tile([P, 1], F32, name="scratch")
         nc.vector.memset(scratch[:], 0.0)
         warmed = held.tile([P, 1], F32, name="warmed")
         nc.scalar.activation(warmed[:], scratch[:], ACT.Exp)
 
-        minus_bias = held.tile([P, GROUPS, BLOCKS], F32, name="minus_bias")
-        nc.vector.tensor_scalar_mul(minus_bias[:], bias[:], -1.0)
-
         for g in range(GROUPS):
-            w_blocks = w_sb[g][:].rearrange("p h (m i) -> p h i m", i=BLOCKS)
-            for i in range(BLOCKS):
+            w_blocks = w_sb[g][:].rearrange("p h (m i) -> p h i m", i=GROUP_BLOCKS[g])
+            for i in range(GROUP_BLOCKS[g]):
                 product = psum.tile([P, N], F32, name="product")
                 for h in range(HALVES):
                     nc.tensor.matmul(
@@ -68,28 +70,23 @@ def tile_mthisan_kernel(tc, base, x, w, b, offs, out):
                         stop=(h == HALVES - 1),
                     )
 
+                exp_v = work.tile([P, N], F32, name="exp_v")
+                nc.scalar.activation(exp_v[:], product[:], ACT.Exp, bias=bias[g][:, i : i + 1])
                 positive_part = work.tile([P, N], F32, name="positive_part")
+                nc.scalar.activation(
+                    positive_part[:], product[:], ACT.Relu, bias=bias[g][:, i : i + 1]
+                )
                 negative_part = work.tile([P, N], F32, name="negative_part")
                 if g == 0 and i == 0:
-                    exp_v = work.tile([P, N], F32, name="exp_v")
-                    nc.scalar.activation(exp_v[:], product[:], ACT.Exp, bias=bias[:, g, i : i + 1])
-                    nc.scalar.activation(
-                        positive_part[:], product[:], ACT.Relu, bias=bias[:, g, i : i + 1]
-                    )
                     nc.vector.tensor_scalar(
                         negative_part[:], exp_v[:], 1.0, -1.0, op0=ALU.min, op1=ALU.add
                     )
                 else:
-                    minus_min = work.tile([P, N], F32, name="minus_min")
+                    minus_negative = work.tile([P, N], F32, name="minus_negative")
                     nc.scalar.activation(
-                        minus_min[:], product[:], ACT.Relu, bias=minus_bias[:, g, i : i + 1], scale=-1.0
+                        minus_negative[:], exp_v[:], ACT.Relu, bias=1.0, scale=-1.0
                     )
-                    exp_min = work.tile([P, N], F32, name="exp_min")
-                    nc.scalar.activation(exp_min[:], minus_min[:], ACT.Exp, scale=-1.0)
-                    nc.scalar.activation(
-                        positive_part[:], product[:], ACT.Relu, bias=bias[:, g, i : i + 1]
-                    )
-                    nc.scalar.activation(negative_part[:], exp_min[:], ACT.Copy, bias=-1.0)
+                    nc.scalar.activation(negative_part[:], minus_negative[:], ACT.Copy, scale=-1.0)
 
                 nc.vector.tensor_tensor(
                     windows[g][i][:].indirect(offsets[:]),
@@ -97,4 +94,4 @@ def tile_mthisan_kernel(tc, base, x, w, b, offs, out):
                     negative_part[:],
                     ALU.add,
                 )
-                nc.sync.dma_start(out_blocks[:, g, i, :], windows[g][i][:])
+                nc.sync.dma_start(rows_of_group(out, g)[:, i, :], windows[g][i][:])

@@ -10,7 +10,7 @@ P = 128
 C, S, N, E = 1024, 256, 128, 256
 HALVES = E // P
 ALL_BLOCKS = C // P
-GROUP_BLOCKS = (2, 6)
+GROUP_BLOCKS = (2, 2, 4)
 GROUPS = len(GROUP_BLOCKS)
 
 FLOPS = 2 * E * C * N
@@ -45,10 +45,14 @@ def tile_mthisan_kernel(tc, base, x, w, b, offs, out):
         nc.sync.dma_start(w_sb[0][:], w_rows[:, :, first[0] : first[1]])
         nc.scalar.dma_start(x_sb[:], x.rearrange("(p h) n -> p h n", p=P))
         nc.scalar.dma_start(bias[0][:], rows_of_group(b, 0).rearrange("p i o -> p (i o)"))
-        nc.sync.dma_start(offsets[:], offs)
-        nc.sync.dma_start(w_sb[1][:], w_rows[:, :, first[1] : first[2]])
-        nc.scalar.dma_start(bias[1][:], rows_of_group(b, 1).rearrange("p i o -> p (i o)"))
         for g in range(GROUPS):
+            if g + 1 < GROUPS:
+                nc.sync.dma_start(w_sb[g + 1][:], w_rows[:, :, first[g + 1] : first[g + 2]])
+                nc.sync.dma_start(
+                    bias[g + 1][:], rows_of_group(b, g + 1).rearrange("p i o -> p (i o)")
+                )
+            if g == 0:
+                nc.sync.dma_start(offsets[:], offs)
             for i in range(GROUP_BLOCKS[g]):
                 nc.sync.dma_start(windows[g][i][:], rows_of_group(base, g)[:, i, :])
 

@@ -77,15 +77,19 @@ def tile_mthisan_kernel(tc, base, x, w, b, offs, out):
                 exp_v = work.tile([P, N], F32, name="exp_v")
                 nc.scalar.activation(exp_v[:], product[:], ACT.Exp, bias=bias[g][:, i : i + 1])
                 positive_part = work.tile([P, N], F32, name="positive_part")
-                nc.scalar.activation(
-                    positive_part[:], product[:], ACT.Relu, bias=bias[g][:, i : i + 1]
-                )
                 negative_part = work.tile([P, N], F32, name="negative_part")
                 if g == 0 and i == 0:
+                    nc.vector.tensor_scalar(
+                        positive_part[:], product[:], bias[g][:, i : i + 1], 0.0,
+                        op0=ALU.add, op1=ALU.max,
+                    )
                     nc.vector.tensor_scalar(
                         negative_part[:], exp_v[:], 1.0, -1.0, op0=ALU.min, op1=ALU.add
                     )
                 else:
+                    nc.scalar.activation(
+                        positive_part[:], product[:], ACT.Relu, bias=bias[g][:, i : i + 1]
+                    )
                     minus_negative = work.tile([P, N], F32, name="minus_negative")
                     nc.scalar.activation(
                         minus_negative[:], exp_v[:], ACT.Relu, bias=1.0, scale=-1.0

@@ -63,6 +63,7 @@ def tile_mthisan_kernel(tc, base, x, w, b, offs, out):
 
         for g in range(GROUPS):
             w_blocks = w_sb[g][:].rearrange("p h (m i) -> p h i m", i=GROUP_BLOCKS[g])
+            parts = []
             for i in range(GROUP_BLOCKS[g]):
                 product = psum.tile([P, N], F32, name="product")
                 for h in range(HALVES):
@@ -74,28 +75,30 @@ def tile_mthisan_kernel(tc, base, x, w, b, offs, out):
                         stop=(h == HALVES - 1),
                     )
 
+                bias_i = bias[g][:, i : i + 1]
                 exp_v = work.tile([P, N], F32, name="exp_v")
-                nc.scalar.activation(exp_v[:], product[:], ACT.Exp, bias=bias[g][:, i : i + 1])
+                nc.scalar.activation(exp_v[:], product[:], ACT.Exp, bias=bias_i)
                 positive_part = work.tile([P, N], F32, name="positive_part")
-                negative_part = work.tile([P, N], F32, name="negative_part")
                 if g == 0 and i == 0:
                     nc.vector.tensor_scalar(
-                        positive_part[:], product[:], bias[g][:, i : i + 1], 0.0,
-                        op0=ALU.add, op1=ALU.max,
+                        positive_part[:], product[:], bias_i, 0.0, op0=ALU.add, op1=ALU.max
                     )
+                else:
+                    nc.scalar.activation(positive_part[:], product[:], ACT.Relu, bias=bias_i)
+                negative_part = work.tile([P, N], F32, name="negative_part")
+                if g == 0:
                     nc.vector.tensor_scalar(
                         negative_part[:], exp_v[:], 1.0, -1.0, op0=ALU.min, op1=ALU.add
                     )
                 else:
-                    nc.scalar.activation(
-                        positive_part[:], product[:], ACT.Relu, bias=bias[g][:, i : i + 1]
-                    )
                     minus_negative = work.tile([P, N], F32, name="minus_negative")
                     nc.scalar.activation(
                         minus_negative[:], exp_v[:], ACT.Relu, bias=1.0, scale=-1.0
                     )
                     nc.scalar.activation(negative_part[:], minus_negative[:], ACT.Copy, scale=-1.0)
+                parts.append((positive_part, negative_part))
 
+            for i, (positive_part, negative_part) in enumerate(parts):
                 nc.vector.tensor_tensor(
                     windows[g][i][:].indirect(offsets[:]),
                     positive_part[:],

import concourse.mybir as mybir

F32 = mybir.dt.float32
BF16 = mybir.dt.bfloat16
U16 = mybir.dt.uint16
ACT = mybir.ActivationFunctionType
ALU = mybir.AluOpType

P = 128
C, S, N, E = 1024, 256, 128, 256
HALVES = E // P
ALL_BLOCKS = C // P
GROUP_BLOCKS = (2, 2, 4)
GROUPS = len(GROUP_BLOCKS)

FLOPS = 2 * E * C * N


def tile_mthisan_kernel(tc, base, x, w, b, offs, out):
    nc = tc.nc

    first = [P * sum(GROUP_BLOCKS[:g]) for g in range(GROUPS + 1)]
    w_rows = w.rearrange("(p h) c -> p h c", p=P)

    def rows_of_group(array, g):
        return array[first[g] : first[g + 1], :].rearrange("(p i) s -> p i s", p=P)

    with (
        tc.tile_pool(name="held", bufs=1) as held,
        tc.tile_pool(name="work", bufs=ALL_BLOCKS) as work,
        tc.psum_pool(name="psum", bufs=ALL_BLOCKS) as psum,
    ):
        offsets = held.tile([P, N // 16], U16, name="offsets")
        x_sb = held.tile([P, HALVES, N], BF16, name="x_sb")
        bias = [held.tile([P, GROUP_BLOCKS[g]], F32, name=f"bias{g}") for g in range(GROUPS)]
        w_sb = [
            held.tile([P, HALVES, P * GROUP_BLOCKS[g]], BF16, name=f"w_sb{g}")
            for g in range(GROUPS)
        ]
        windows = [
            [held.tile([P, S], F32, name=f"window{g}_{i}") for i in range(GROUP_BLOCKS[g])]
            for g in range(GROUPS)
        ]

        nc.sync.dma_start(w_sb[0][:], w_rows[:, :, first[0] : first[1]])
        nc.scalar.dma_start(x_sb[:], x.rearrange("(p h) n -> p h n", p=P))
        nc.scalar.dma_start(bias[0][:], rows_of_group(b, 0).rearrange("p i o -> p (i o)"))
        for g in range(GROUPS):
            if g + 1 < GROUPS:
                nc.sync.dma_start(w_sb[g + 1][:], w_rows[:, :, first[g + 1] : first[g + 2]])
                nc.sync.dma_start(
                    bias[g + 1][:], rows_of_group(b, g + 1).rearrange("p i o -> p (i o)")
                )
            if g == 0:
                nc.sync.dma_start(offsets[:], offs)
            for i in range(GROUP_BLOCKS[g]):
                nc.sync.dma_start(windows[g][i][:], rows_of_group(base, g)[:, i, :])

        scratch = held.tile([P, 1], F32, name="scratch")
        nc.vector.memset(scratch[:], 0.0)
        warmed = held.tile([P, 1], F32, name="warmed")
        nc.scalar.activation(warmed[:], scratch[:], ACT.Exp)

        for g in range(GROUPS):
            w_blocks = w_sb[g][:].rearrange("p h (m i) -> p h i m", i=GROUP_BLOCKS[g])
            parts = []
            for i in range(GROUP_BLOCKS[g]):
                product = psum.tile([P, N], F32, name="product")
                for h in range(HALVES):
                    nc.tensor.matmul(
                        product[:],
                        w_blocks[:, h, i, :],
                        x_sb[:, h, :],
                        start=(h == 0),
                        stop=(h == HALVES - 1),
                    )

                bias_i = bias[g][:, i : i + 1]
                exp_v = work.tile([P, N], F32, name="exp_v")
                nc.scalar.activation(exp_v[:], product[:], ACT.Exp, bias=bias_i)
                positive_part = work.tile([P, N], F32, name="positive_part")
                if g == 0 and i == 0:
                    nc.vector.tensor_scalar(
                        positive_part[:], product[:], bias_i, 0.0, op0=ALU.add, op1=ALU.max
                    )
                else:
                    nc.scalar.activation(positive_part[:], product[:], ACT.Relu, bias=bias_i)
                negative_part = work.tile([P, N], F32, name="negative_part")
                if g == 0:
                    nc.vector.tensor_scalar(
                        negative_part[:], exp_v[:], 1.0, -1.0, op0=ALU.min, op1=ALU.add
                    )
                else:
                    minus_negative = work.tile([P, N], F32, name="minus_negative")
                    nc.scalar.activation(
                        minus_negative[:], exp_v[:], ACT.Relu, bias=1.0, scale=-1.0
                    )
                    nc.scalar.activation(negative_part[:], minus_negative[:], ACT.Copy, scale=-1.0)
                parts.append((positive_part, negative_part))

            for i, (positive_part, negative_part) in enumerate(parts):
                nc.vector.tensor_tensor(
                    windows[g][i][:].indirect(offsets[:]),
                    positive_part[:],
                    negative_part[:],
                    ALU.add,
                )
                nc.sync.dma_start(rows_of_group(out, g)[:, i, :], windows[g][i][:])
